import numpy as np
import ml_dtypes

BF16 = ml_dtypes.bfloat16


def bf(x):
    return np.asarray(x, np.float32).astype(BF16)


def f32(x):
    return np.asarray(x, np.float32)


def f64(x):
    return np.asarray(x).astype(np.float64)


def striped(idx):
    return np.tile(idx.reshape(-1, 16).T, (8, 1))


D, S, M, N = 128, 4096, 256, 1024
VEHICLE_CAP = 1.0
BATTERY_CAP = 1.0


def setup_inputs():
    return {
        "table": bf(np.random.standard_normal((D, S))),
        "w": bf(np.random.standard_normal((D, M)) / np.sqrt(D)),
        "w_context": bf(0.5 * np.random.standard_normal((D, M))),
        "w_cap": f32(0.5 * np.random.standard_normal((M, 1))),
        "w_bat": f32(0.5 * np.random.standard_normal((M, 1))),
        "w_time": f32(0.5 * np.random.standard_normal((M, 1))),
        "used_capacity": f32(np.random.uniform(size=(1, N))),
        "used_battery": f32(np.random.uniform(size=(1, N))),
        "current_time": f32(np.random.uniform(size=(1, N))),
        "offs": striped(np.random.permutation(np.tile(np.arange(S), 2))[:N]),
    }


def reference(table, w, w_context, w_cap, w_bat, w_time, used_capacity, used_battery, current_time, offs):
    idx = offs[:16].T.reshape(-1)
    ctx = (f64(w_context).T @ f64(table)).mean(axis=1, keepdims=True)
    state = f64(w_cap) * (VEHICLE_CAP - f64(used_capacity)) + f64(w_bat) * (BATTERY_CAP - f64(used_battery)) + f64(w_time) * f64(current_time)
    return f64(w).T @ f64(table)[:, idx] + ctx + state

@@ -1,0 +1,95 @@
+import concourse.mybir as mybir
+
+BF16, F32, U16 = mybir.dt.bfloat16, mybir.dt.float32, mybir.dt.uint16
+ALU = mybir.AluOpType
+ACT = mybir.ActivationFunctionType
+AXIS = mybir.AxisListType
+
+P = 128
+NODES = 4096
+M = 256
+N = 1024
+BLOCKS = M // P
+PIECE = 512
+PIECES = N // PIECE
+CHUNK = 1024
+CHUNKS = NODES // CHUNK
+TERMS = 3
+
+FLOPS = 2 * P * M * N + P * NODES + 2 * P * M + 2 * TERMS * M * N
+
+
+def tile_decoder_my_kernel(
+    tc, table, w, w_context, w_cap, w_bat, w_time, used_capacity, used_battery, current_time, offs, out
+):
+    nc = tc.nc
+    with (
+        tc.tile_pool(name="held", bufs=1) as held,
+        tc.tile_pool(name="results", bufs=4) as results,
+        tc.psum_pool(name="psum", bufs=1) as psum,
+    ):
+        offsets = held.tile([P, N // 16], U16, name="offsets")
+        nc.sync.dma_start(offsets[:], offs)
+
+        used = held.tile([2, N], F32, name="used")
+        state_rows = held.tile([TERMS, N], F32, name="state_rows")
+        nc.scalar.dma_start(used[0:1, :], used_capacity)
+        nc.scalar.dma_start(used[1:2, :], used_battery)
+        nc.scalar.dma_start(state_rows[2:3, :], current_time)
+
+        state_w = held.tile([TERMS, M], F32, name="state_w")
+        for row, vector in enumerate((w_cap, w_bat, w_time)):
+            nc.scalar.dma_start(state_w[row : row + 1, :], vector.rearrange("m o -> o m"))
+
+        w_context_sb = held.tile([P, M], BF16, name="w_context_sb")
+        nc.scalar.dma_start(w_context_sb[:], w_context)
+        w_sb = held.tile([P, M], BF16, name="w_sb")
+        nc.scalar.dma_start(w_sb[:], w)
+
+        table_sb = held.tile([P, NODES], BF16, name="table_sb")
+        for c in range(CHUNKS):
+            nc.sync.dma_start(table_sb[:, c * CHUNK : (c + 1) * CHUNK], table[:, c * CHUNK : (c + 1) * CHUNK])
+
+        nc.vector.tensor_scalar(state_rows[0:2, :], used[:], -1.0, 1.0, ALU.mult, ALU.add)
+
+        banks = {}
+        for piece in range(PIECES):
+            for block in range(BLOCKS):
+                banks[piece, block] = psum.tile([P, PIECE], F32, name=f"bank{piece}{block}")
+                nc.tensor.matmul(
+                    banks[piece, block][:],
+                    state_w[:, block * P : (block + 1) * P],
+                    state_rows[:, piece * PIECE : (piece + 1) * PIECE],
+                    start=True,
+                    stop=False,
+                )
+
+        w_mean = held.tile([P, M], F32, name="w_mean")
+        nc.scalar.activation(w_mean[:], w_context_sb[:], ACT.Copy, scale=1.0 / NODES)
+        node_sums = held.tile([P, CHUNKS], F32, name="node_sums")
+        for c in range(CHUNKS):
+            nc.vector.reduce_sum(node_sums[:, c : c + 1], table_sb[:, c * CHUNK : (c + 1) * CHUNK], axis=AXIS.X)
+        ctx_parts = psum.tile([P, BLOCKS, CHUNKS], F32, name="ctx_parts")
+        for block in range(BLOCKS):
+            nc.tensor.matmul(ctx_parts[:, block, :], w_mean[:, block * P : (block + 1) * P], node_sums[:])
+        ctx = held.tile([P, BLOCKS], F32, name="ctx")
+        nc.vector.reduce_sum(ctx[:], ctx_parts[:], axis=AXIS.X)
+
+        for piece in range(PIECES):
+            for block in range(BLOCKS):
+                bank = banks[piece, block]
+                nc.tensor.matmul(
+                    bank[:],
+                    w_sb[:, block * P : (block + 1) * P],
+                    table_sb[:].indirect(offsets[:, piece * (PIECE // 16) : (piece + 1) * (PIECE // 16)]),
+                    start=False,
+                    stop=True,
+                )
+                result = results.tile([P, PIECE], F32, name="result")
+                out_part = out[block * P : (block + 1) * P, piece * PIECE : (piece + 1) * PIECE]
+                if block == 0:
+                    nc.vector.tensor_scalar_add(result[:], bank[:], ctx[:, 0:1])
+                    nc.sync.dma_start(out_part, result[:])
+                else:
+                    nc.scalar.activation(result[:], bank[:], ACT.Identity, bias=ctx[:, 1:2])
+                    nc.scalar.dma_start(out_part, result[:])

@@ -28,29 +28,39 @@ def tile_decoder_my_kernel(
         tc.tile_pool(name="results", bufs=4) as results,
         tc.psum_pool(name="psum", bufs=1) as psum,
     ):
-        offsets = held.tile([P, N // 16], U16, name="offsets")
-        nc.sync.dma_start(offsets[:], offs)
+        state_w = held.tile([P, M], F32, name="state_w")
+        nc.vector.memset(state_w[:], 0.0)
+        state_rows = held.tile([P, N], F32, name="state_rows")
+        nc.gpsimd.memset(state_rows[:], 0.0)
 
-        used = held.tile([2, N], F32, name="used")
-        state_rows = held.tile([TERMS, N], F32, name="state_rows")
-        nc.scalar.dma_start(used[0:1, :], used_capacity)
-        nc.scalar.dma_start(used[1:2, :], used_battery)
-        nc.scalar.dma_start(state_rows[2:3, :], current_time)
-
-        state_w = held.tile([TERMS, M], F32, name="state_w")
-        for row, vector in enumerate((w_cap, w_bat, w_time)):
-            nc.scalar.dma_start(state_w[row : row + 1, :], vector.rearrange("m o -> o m"))
-
-        w_context_sb = held.tile([P, M], BF16, name="w_context_sb")
-        nc.scalar.dma_start(w_context_sb[:], w_context)
-        w_sb = held.tile([P, M], BF16, name="w_sb")
-        nc.scalar.dma_start(w_sb[:], w)
+        queues = (nc.sync, nc.scalar, nc.gpsimd)
+        loaded_rows = held.tile([TERMS, N], F32, name="loaded_rows")
+        for term, row in enumerate((used_capacity, used_battery, current_time)):
+            queues[term].dma_start(loaded_rows[term : term + 1, :], row)
+        for term, vector in enumerate((w_cap, w_bat, w_time)):
+            queues[term].dma_start(state_w[term : term + 1, :], vector.rearrange("m o -> o m"))
 
         table_sb = held.tile([P, NODES], BF16, name="table_sb")
         for c in range(CHUNKS):
-            nc.sync.dma_start(table_sb[:, c * CHUNK : (c + 1) * CHUNK], table[:, c * CHUNK : (c + 1) * CHUNK])
+            queues[c % 2].dma_start(table_sb[:, c * CHUNK : (c + 1) * CHUNK], table[:, c * CHUNK : (c + 1) * CHUNK])
+        offsets = held.tile([P, N // 16], U16, name="offsets")
+        nc.sync.dma_start(offsets[:], offs)
+        w_context_sb = held.tile([P, M], BF16, name="w_context_sb")
+        nc.gpsimd.dma_start(w_context_sb[:], w_context)
+        w_sb = held.tile([P, M], BF16, name="w_sb")
+        nc.gpsimd.dma_start(w_sb[:], w)
 
-        nc.vector.tensor_scalar(state_rows[0:2, :], used[:], -1.0, 1.0, ALU.mult, ALU.add)
+        slope = held.tile([TERMS, 1], F32, name="slope")
+        nc.vector.memset(slope[:], 1.0)
+        nc.vector.memset(slope[0:2, :], -1.0)
+        shift = held.tile([TERMS, 1], F32, name="shift")
+        nc.vector.memset(shift[:], 0.0)
+        nc.vector.memset(shift[0:2, :], 1.0)
+        for piece in range(PIECES):
+            columns = slice(piece * PIECE, (piece + 1) * PIECE)
+            nc.vector.tensor_scalar(
+                state_rows[0:TERMS, columns], loaded_rows[:, columns], slope[:], shift[:], ALU.mult, ALU.add
+            )
 
         banks = {}
         for piece in range(PIECES):

@@ -26,19 +26,20 @@ def tile_decoder_my_kernel(
     with (
         tc.tile_pool(name="held", bufs=1) as held,
         tc.tile_pool(name="results", bufs=4) as results,
+        tc.tile_pool(name="scratch", bufs=2) as scratch,
         tc.psum_pool(name="psum", bufs=1) as psum,
     ):
         state_w = held.tile([P, M], F32, name="state_w")
         nc.vector.memset(state_w[:], 0.0)
         state_rows = held.tile([P, N], F32, name="state_rows")
-        nc.gpsimd.memset(state_rows[:], 0.0)
+        nc.vector.memset(state_rows[:], 0.0)
 
-        queues = (nc.sync, nc.scalar, nc.gpsimd)
+        queues = (nc.sync, nc.scalar)
         loaded_rows = held.tile([TERMS, N], F32, name="loaded_rows")
         for term, row in enumerate((used_capacity, used_battery, current_time)):
-            queues[term].dma_start(loaded_rows[term : term + 1, :], row)
+            queues[term % 2].dma_start(loaded_rows[term : term + 1, :], row)
         for term, vector in enumerate((w_cap, w_bat, w_time)):
-            queues[term].dma_start(state_w[term : term + 1, :], vector.rearrange("m o -> o m"))
+            queues[(TERMS + term) % 2].dma_start(state_w[term : term + 1, :], vector.rearrange("m o -> o m"))
 
         table_sb = held.tile([P, NODES], BF16, name="table_sb")
         for c in range(CHUNKS):
@@ -46,9 +47,9 @@ def tile_decoder_my_kernel(
         offsets = held.tile([P, N // 16], U16, name="offsets")
         nc.sync.dma_start(offsets[:], offs)
         w_context_sb = held.tile([P, M], BF16, name="w_context_sb")
-        nc.gpsimd.dma_start(w_context_sb[:], w_context)
+        nc.scalar.dma_start(w_context_sb[:], w_context)
         w_sb = held.tile([P, M], BF16, name="w_sb")
-        nc.gpsimd.dma_start(w_sb[:], w)
+        nc.sync.dma_start(w_sb[:], w)
 
         slope = held.tile([TERMS, 1], F32, name="slope")
         nc.vector.memset(slope[:], 1.0)
@@ -78,7 +79,16 @@ def tile_decoder_my_kernel(
         nc.scalar.activation(w_mean[:], w_context_sb[:], ACT.Copy, scale=1.0 / NODES)
         node_sums = held.tile([P, CHUNKS], F32, name="node_sums")
         for c in range(CHUNKS):
-            nc.vector.reduce_sum(node_sums[:, c : c + 1], table_sb[:, c * CHUNK : (c + 1) * CHUNK], axis=AXIS.X)
+            unread = scratch.tile([P, CHUNK], BF16, name="unread")
+            nc.vector.tensor_scalar(
+                unread[:],
+                table_sb[:, c * CHUNK : (c + 1) * CHUNK],
+                1.0,
+                None,
+                ALU.mult,
+                ALU.add,
+                accum_out=node_sums[:, c : c + 1],
+            )
         ctx_parts = psum.tile([P, BLOCKS, CHUNKS], F32, name="ctx_parts")
         for block in range(BLOCKS):
             nc.tensor.matmul(ctx_parts[:, block, :], w_mean[:, block * P : (block + 1) * P], node_sums[:])

@@ -15,6 +15,7 @@ PIECES = N // PIECE
 CHUNK = 1024
 CHUNKS = NODES // CHUNK
 TERMS = 3
+WARM_UPS = 6
 
 FLOPS = 2 * P * M * N + P * NODES + 2 * P * M + 2 * TERMS * M * N
 
@@ -29,6 +30,12 @@ def tile_decoder_my_kernel(
         tc.tile_pool(name="scratch", bufs=2) as scratch,
         tc.psum_pool(name="psum", bufs=1) as psum,
     ):
+        zeros = held.tile([P, PIECE], BF16, name="zeros")
+        nc.gpsimd.memset(zeros[:], 0.0)
+        unread_bank = psum.tile([P, PIECE], F32, name="unread_bank")
+        for repeat in range(WARM_UPS):
+            nc.tensor.matmul(unread_bank[:], zeros[:, 0:P], zeros[:])
+
         state_w = held.tile([P, M], F32, name="state_w")
         nc.vector.memset(state_w[:], 0.0)
         state_rows = held.tile([P, N], F32, name="state_rows")

@@ -15,7 +15,7 @@ PIECES = N // PIECE
 CHUNK = 1024
 CHUNKS = NODES // CHUNK
 TERMS = 3
-WARM_UPS = 6
+WARM_UPS = 16
 
 FLOPS = 2 * P * M * N + P * NODES + 2 * P * M + 2 * TERMS * M * N
 
@@ -30,11 +30,11 @@ def tile_decoder_my_kernel(
         tc.tile_pool(name="scratch", bufs=2) as scratch,
         tc.psum_pool(name="psum", bufs=1) as psum,
     ):
-        zeros = held.tile([P, PIECE], BF16, name="zeros")
+        zeros = held.tile([P, P], BF16, name="zeros")
         nc.gpsimd.memset(zeros[:], 0.0)
-        unread_bank = psum.tile([P, PIECE], F32, name="unread_bank")
+        unread_bank = psum.tile([P, P], F32, name="unread_bank")
         for repeat in range(WARM_UPS):
-            nc.tensor.matmul(unread_bank[:], zeros[:, 0:P], zeros[:])
+            nc.tensor.matmul(unread_bank[:], zeros[:], zeros[:])
 
         state_w = held.tile([P, M], F32, name="state_w")
         nc.vector.memset(state_w[:], 0.0)

@@ -41,16 +41,16 @@ def tile_decoder_my_kernel(
         state_rows = held.tile([P, N], F32, name="state_rows")
         nc.vector.memset(state_rows[:], 0.0)
 
-        queues = (nc.sync, nc.scalar)
         loaded_rows = held.tile([TERMS, N], F32, name="loaded_rows")
-        for term, row in enumerate((used_capacity, used_battery, current_time)):
-            queues[term % 2].dma_start(loaded_rows[term : term + 1, :], row)
+        nc.sync.dma_start(loaded_rows[0:1, :], used_capacity)
+        nc.scalar.dma_start(loaded_rows[1:2, :], used_battery)
+        nc.sync.dma_start(loaded_rows[2:3, :], current_time)
         for term, vector in enumerate((w_cap, w_bat, w_time)):
-            queues[(TERMS + term) % 2].dma_start(state_w[term : term + 1, :], vector.rearrange("m o -> o m"))
+            nc.scalar.dma_start(state_w[term : term + 1, :], vector.rearrange("m o -> o m"))
 
         table_sb = held.tile([P, NODES], BF16, name="table_sb")
         for c in range(CHUNKS):
-            queues[c % 2].dma_start(table_sb[:, c * CHUNK : (c + 1) * CHUNK], table[:, c * CHUNK : (c + 1) * CHUNK])
+            nc.sync.dma_start(table_sb[:, c * CHUNK : (c + 1) * CHUNK], table[:, c * CHUNK : (c + 1) * CHUNK])
         offsets = held.tile([P, N // 16], U16, name="offsets")
         nc.sync.dma_start(offsets[:], offs)
         w_context_sb = held.tile([P, M], BF16, name="w_context_sb")

@@ -45,8 +45,9 @@ def tile_decoder_my_kernel(
         nc.sync.dma_start(loaded_rows[0:1, :], used_capacity)
         nc.scalar.dma_start(loaded_rows[1:2, :], used_battery)
         nc.sync.dma_start(loaded_rows[2:3, :], current_time)
-        for term, vector in enumerate((w_cap, w_bat, w_time)):
-            nc.scalar.dma_start(state_w[term : term + 1, :], vector.rearrange("m o -> o m"))
+        nc.sync.dma_start(state_w[0:1, :], w_cap.rearrange("m o -> o m"))
+        nc.scalar.dma_start(state_w[1:2, :], w_bat.rearrange("m o -> o m"))
+        nc.sync.dma_start(state_w[2:3, :], w_time.rearrange("m o -> o m"))
 
         table_sb = held.tile([P, NODES], BF16, name="table_sb")
         for c in range(CHUNKS):

@@ -120,4 +120,4 @@ def tile_decoder_my_kernel(
                     nc.sync.dma_start(out_part, result[:])
                 else:
                     nc.scalar.activation(result[:], bank[:], ACT.Identity, bias=ctx[:, 1:2])
-                    nc.scalar.dma_start(out_part, result[:])
+                    nc.sync.dma_start(out_part, result[:])

import concourse.mybir as mybir

BF16, F32, U16 = mybir.dt.bfloat16, mybir.dt.float32, mybir.dt.uint16
ALU = mybir.AluOpType
ACT = mybir.ActivationFunctionType
AXIS = mybir.AxisListType

P = 128
NODES = 4096
M = 256
N = 1024
BLOCKS = M // P
PIECE = 512
PIECES = N // PIECE
CHUNK = 1024
CHUNKS = NODES // CHUNK
TERMS = 3
WARM_UPS = 16

FLOPS = 2 * P * M * N + P * NODES + 2 * P * M + 2 * TERMS * M * N


def tile_decoder_my_kernel(
    tc, table, w, w_context, w_cap, w_bat, w_time, used_capacity, used_battery, current_time, offs, out
):
    nc = tc.nc
    with (
        tc.tile_pool(name="held", bufs=1) as held,
        tc.tile_pool(name="results", bufs=4) as results,
        tc.tile_pool(name="scratch", bufs=2) as scratch,
        tc.psum_pool(name="psum", bufs=1) as psum,
    ):
        zeros = held.tile([P, P], BF16, name="zeros")
        nc.gpsimd.memset(zeros[:], 0.0)
        unread_bank = psum.tile([P, P], F32, name="unread_bank")
        for repeat in range(WARM_UPS):
            nc.tensor.matmul(unread_bank[:], zeros[:], zeros[:])

        state_w = held.tile([P, M], F32, name="state_w")
        nc.vector.memset(state_w[:], 0.0)
        state_rows = held.tile([P, N], F32, name="state_rows")
        nc.vector.memset(state_rows[:], 0.0)

        loaded_rows = held.tile([TERMS, N], F32, name="loaded_rows")
        nc.sync.dma_start(loaded_rows[0:1, :], used_capacity)
        nc.scalar.dma_start(loaded_rows[1:2, :], used_battery)
        nc.sync.dma_start(loaded_rows[2:3, :], current_time)
        nc.sync.dma_start(state_w[0:1, :], w_cap.rearrange("m o -> o m"))
        nc.scalar.dma_start(state_w[1:2, :], w_bat.rearrange("m o -> o m"))
        nc.sync.dma_start(state_w[2:3, :], w_time.rearrange("m o -> o m"))

        table_sb = held.tile([P, NODES], BF16, name="table_sb")
        for c in range(CHUNKS):
            nc.sync.dma_start(table_sb[:, c * CHUNK : (c + 1) * CHUNK], table[:, c * CHUNK : (c + 1) * CHUNK])
        offsets = held.tile([P, N // 16], U16, name="offsets")
        nc.sync.dma_start(offsets[:], offs)
        w_context_sb = held.tile([P, M], BF16, name="w_context_sb")
        nc.scalar.dma_start(w_context_sb[:], w_context)
        w_sb = held.tile([P, M], BF16, name="w_sb")
        nc.sync.dma_start(w_sb[:], w)

        slope = held.tile([TERMS, 1], F32, name="slope")
        nc.vector.memset(slope[:], 1.0)
        nc.vector.memset(slope[0:2, :], -1.0)
        shift = held.tile([TERMS, 1], F32, name="shift")
        nc.vector.memset(shift[:], 0.0)
        nc.vector.memset(shift[0:2, :], 1.0)
        for piece in range(PIECES):
            columns = slice(piece * PIECE, (piece + 1) * PIECE)
            nc.vector.tensor_scalar(
                state_rows[0:TERMS, columns], loaded_rows[:, columns], slope[:], shift[:], ALU.mult, ALU.add
            )

        banks = {}
        for piece in range(PIECES):
            for block in range(BLOCKS):
                banks[piece, block] = psum.tile([P, PIECE], F32, name=f"bank{piece}{block}")
                nc.tensor.matmul(
                    banks[piece, block][:],
                    state_w[:, block * P : (block + 1) * P],
                    state_rows[:, piece * PIECE : (piece + 1) * PIECE],
                    start=True,
                    stop=False,
                )

        w_mean = held.tile([P, M], F32, name="w_mean")
        nc.scalar.activation(w_mean[:], w_context_sb[:], ACT.Copy, scale=1.0 / NODES)
        node_sums = held.tile([P, CHUNKS], F32, name="node_sums")
        for c in range(CHUNKS):
            unread = scratch.tile([P, CHUNK], BF16, name="unread")
            nc.vector.tensor_scalar(
                unread[:],
                table_sb[:, c * CHUNK : (c + 1) * CHUNK],
                1.0,
                None,
                ALU.mult,
                ALU.add,
                accum_out=node_sums[:, c : c + 1],
            )
        ctx_parts = psum.tile([P, BLOCKS, CHUNKS], F32, name="ctx_parts")
        for block in range(BLOCKS):
            nc.tensor.matmul(ctx_parts[:, block, :], w_mean[:, block * P : (block + 1) * P], node_sums[:])
        ctx = held.tile([P, BLOCKS], F32, name="ctx")
        nc.vector.reduce_sum(ctx[:], ctx_parts[:], axis=AXIS.X)

        for piece in range(PIECES):
            for block in range(BLOCKS):
                bank = banks[piece, block]
                nc.tensor.matmul(
                    bank[:],
                    w_sb[:, block * P : (block + 1) * P],
                    table_sb[:].indirect(offsets[:, piece * (PIECE // 16) : (piece + 1) * (PIECE // 16)]),
                    start=False,
                    stop=True,
                )
                result = results.tile([P, PIECE], F32, name="result")
                out_part = out[block * P : (block + 1) * P, piece * PIECE : (piece + 1) * PIECE]
                if block == 0:
                    nc.vector.tensor_scalar_add(result[:], bank[:], ctx[:, 0:1])
                    nc.sync.dma_start(out_part, result[:])
                else:
                    nc.scalar.activation(result[:], bank[:], ACT.Identity, bias=ctx[:, 1:2])
                    nc.sync.dma_start(out_part, result[:])
